import numpy as np
import ml_dtypes


def mxq(x, axis, fmt="e4m3"):
    dtype, down = {"e4m3": (ml_dtypes.float8_e4m3fn, 7), "e5m2": (ml_dtypes.float8_e5m2, 14)}[fmt]
    v = np.moveaxis(np.asarray(x, np.float32).astype(ml_dtypes.bfloat16).astype(np.float64), axis, -1)
    blocks = v.reshape(v.shape[:-1] + (-1, 32))
    amax = np.abs(blocks).max(-1, keepdims=True)
    byte = np.maximum(np.where(amax > 0, np.frexp(amax)[1] - 1 + 127, 0) - down, 1)
    scale = np.exp2(byte - 127.0)
    codes = (blocks / scale).astype(np.float32).astype(dtype).astype(np.float64)
    return np.moveaxis((codes * scale).reshape(v.shape), -1, axis)


WIDE = False


def mx_kscale(k):
    if not WIDE:
        return np.ones(k)
    levels = np.array([10, -10, 5, -5, 0])
    a = np.random.permutation(np.resize(levels, k // 512 * 4)).reshape(k // 512, 4)
    idx = np.arange(k)
    return np.exp2(a[idx // 512, idx % 128 // 32])


BF16 = ml_dtypes.bfloat16


def bf(x):
    return np.asarray(x, np.float32).astype(BF16)


def f64(x):
    return np.asarray(x).astype(np.float64)


N, V, EN1, EN2, D, K, EMB = 8192, 4096, 1024, 512, 128, 512, 1024
BN_EPS = 1e-5


def batchnorm(x):
    m = x.mean(axis=0)
    v = x.var(axis=0)
    return (x - m) * (1.0 / np.sqrt(v + BN_EPS))


def setup_inputs():
    s, t = mx_kscale(EN1), mx_kscale(EN2)
    return {
        "en1": bf(np.maximum(np.random.standard_normal((N, EN1)) * 1.15, 0.0) * s),
        "W2": bf(np.random.standard_normal((EN1, EN2)) / np.sqrt(EN1) / s[:, None] * t),
        "b2": bf(np.random.standard_normal(EN2) * 0.2 * t),
        "Wmean": bf(np.random.standard_normal((EN2, D)) / np.sqrt(EN2) / t[:, None]),
        "Wlogvar": bf(np.random.standard_normal((EN2, D)) / np.sqrt(EN2) / t[:, None]),
        "eps": bf(np.random.standard_normal((N, D))),
    }


def reference(en1, W2, b2, Wmean, Wlogvar, eps):
    en2 = np.maximum((mxq(f64(en1), 1, "e4m3") @ mxq(f64(W2), 0, "e4m3")) + f64(b2), 0.0)
    en2q = mxq(en2, 1, "e4m3")
    posterior_mean = batchnorm(en2q @ mxq(f64(Wmean), 0, "e4m3"))
    posterior_logvar = batchnorm(en2q @ mxq(f64(Wlogvar), 0, "e4m3"))
    posterior_var = np.exp(posterior_logvar)
    z = posterior_mean + np.sqrt(posterior_var) * f64(eps)
    zx = batchnorm(z)
    return z, zx

@@ -1,0 +1,373 @@
+from contextlib import ExitStack
+
+import concourse.mybir as mybir
+from concourse.masks import make_identity
+
+F32 = mybir.dt.float32
+BF16 = mybir.dt.bfloat16
+U32 = mybir.dt.uint32
+U8 = mybir.dt.uint8
+FP8X4 = mybir.dt.float8_e4m3fn_x4
+ACT = mybir.ActivationFunctionType
+ALU = mybir.AluOpType
+AXIS = mybir.AxisListType
+
+P = 128
+PACK = 4
+ROWS = 8192
+K1 = 1024
+K2 = 512
+D = 128
+PASSES1 = K1 // (P * PACK)
+BLOCK = 512
+NBLOCKS = ROWS // BLOCK
+SUB = BLOCK // P
+K2_TILES = K2 // P
+WORDS = K1 // 2
+BN_EPS = 1e-5
+BN_STATS_DIM = 6
+LOADS_AHEAD = 3
+
+FLOPS = 2 * ROWS * (K1 * K2 + K2 * 2 * D)
+
+
+def block_cols(j):
+    return slice(j * BLOCK, (j + 1) * BLOCK)
+
+
+def block_rows(dram, j):
+    return dram[j * BLOCK : (j + 1) * BLOCK, :].rearrange("(r s) w -> r (s w)", s=SUB)
+
+
+def regroup(nc, grouped, planes):
+    nc.vector.tensor_copy(
+        out=grouped.rearrange("p (c i) t -> p c t i", i=4),
+        in_=planes.rearrange("p t (c i) -> p c t i", i=4),
+    )
+
+
+def reciprocal_std(nc, pool, variance, minus_half, name):
+    shape = [P, variance.shape[1]]
+    padded = pool.tile(shape, F32, name=name + "_padded")
+    nc.gpsimd.tensor_scalar(
+        out=padded[:], in0=variance, scalar1=1.0, scalar2=BN_EPS, op0=ALU.mult, op1=ALU.add
+    )
+    rstd = pool.tile(shape, F32, name=name)
+    nc.gpsimd.tensor_tensor(
+        out=rstd[:], in0=padded[:], in1=minus_half[:, 0 : shape[1]], op=ALU.pow
+    )
+    return rstd
+
+
+def tile_modelvd_pa_t_kernel(tc, en1, W2, b2, Wmean, Wlogvar, eps, out_0, out_1):
+    nc = tc.nc
+    with ExitStack() as kernel_scope:
+        kernel_scope.enter_context(tc.manual_schedule())
+        keep = kernel_scope.enter_context(tc.tile_pool(name="keep", bufs=1))
+
+        ident_f32 = keep.tile([P, P], F32)
+        make_identity(nc, ident_f32[:])
+        ident_bf16 = keep.tile([P, P], BF16)
+        make_identity(nc, ident_bf16[:])
+        minus_half = keep.tile([P, 2], F32)
+        nc.gpsimd.memset(minus_half[:], -0.5)
+
+        warm = keep.tile([P, 1], F32)
+        nc.vector.memset(warm[:], 0.0)
+        nc.scalar.activation(out=warm[:], in_=warm[:], func=ACT.Exp)
+
+        w2_codes = keep.tile([P, PASSES1, K2], U32, align_bytes=64)
+        w2_scales = keep.tile([P, PASSES1, K2], U8, align_bytes=64)
+        head_codes = keep.tile([P, 2 * D], U32, align_bytes=64)
+        head_scales = keep.tile([P, 2 * D], U8, align_bytes=64)
+        bias = keep.tile([P, K2_TILES], F32)
+        en2_codes = keep.tile([P, ROWS], U32, align_bytes=64)
+        en2_scales = keep.tile([P, ROWS], U8, align_bytes=64)
+        eps_rows = keep.tile([P, NBLOCKS, SUB, D], BF16)
+        stats = keep.tile([P, 2, NBLOCKS, BN_STATS_DIM], F32)
+
+        def second_products(psum, j):
+            products = []
+            for i, name in enumerate(("m_ps", "lv_ps")):
+                product = psum.tile([P, BLOCK], F32, name=name)
+                nc.tensor.matmul_mx(
+                    out=product[:],
+                    lhsT=head_codes[:, i * D : (i + 1) * D].bitcast(FP8X4),
+                    lhsT_scale=head_scales[:, i * D : (i + 1) * D],
+                    rhs=en2_codes[:, block_cols(j)].bitcast(FP8X4),
+                    rhs_scale=en2_scales[:, block_cols(j)],
+                    start=True,
+                    stop=True,
+                )
+                products.append(product)
+            return products
+
+        with ExitStack() as phase:
+            prep = phase.enter_context(tc.tile_pool(name="prep", bufs=1))
+            loads = phase.enter_context(tc.tile_pool(name="loads", bufs=LOADS_AHEAD + 1))
+            work = phase.enter_context(tc.tile_pool(name="work", bufs=2))
+            psum_t = phase.enter_context(tc.psum_pool(name="psum_t", bufs=3))
+            psum_h = phase.enter_context(tc.psum_pool(name="psum_h", bufs=3))
+            psum_s = phase.enter_context(tc.psum_pool(name="psum_s", bufs=1))
+
+            x_of = {}
+            grouped1_of = {}
+            en1_mx_of = {}
+            planes_of = {}
+            grouped2_of = {}
+            products_of = {}
+
+            def load_block(j):
+                x = loads.tile([P, SUB * K1], BF16, name="x")
+                nc.sync.dma_start(out=x[:], in_=block_rows(en1, j))
+                x_of[j] = x
+
+            def transpose_block(j):
+                words = x_of[j][:].bitcast(F32).rearrange("p (s w) -> p s w", s=SUB)
+                grouped1 = work.tile([P, PASSES1 * BLOCK * PACK], BF16, align_bytes=64)
+                pairs = grouped1[:].bitcast(F32).rearrange(
+                    "p (b s r u) -> p b s r u", b=2 * PASSES1, s=2, r=P, u=2
+                )
+                for b in range(2 * PASSES1):
+                    g, half = divmod(b, 2)
+                    xt = psum_t.tile([P, 2, 2, P], F32, tag="xt")
+                    for s in range(2):
+                        for u in range(2):
+                            first = (2 * g + u) * P
+                            nc.tensor.transpose(
+                                xt[:, s, u, :],
+                                words[:, 2 * half + s, first : first + P],
+                                ident_f32[:],
+                            )
+                    permuted = xt[:].rearrange("p s u r -> p s r u")
+                    if b == 2:
+                        nc.vector.tensor_copy(out=pairs[:, b], in_=permuted)
+                    else:
+                        nc.scalar.copy(out=pairs[:, b], in_=permuted)
+                grouped1_of[j] = grouped1
+
+            def quantise_en1(j):
+                codes = work.tile([P, PASSES1 * BLOCK], U32, name="en1_codes", align_bytes=64)
+                scales = work.tile([P, PASSES1 * BLOCK], U8, name="en1_scales", align_bytes=64)
+                nc.vector.quantize_mx(
+                    out=codes[:].bitcast(FP8X4), scales=scales[:], in_=grouped1_of[j][:]
+                )
+                en1_mx_of[j] = (codes, scales)
+
+            def first_product(j):
+                codes, scales = en1_mx_of[j]
+                planes = work.tile([P, K2_TILES, BLOCK], BF16)
+                for t in range(K2_TILES):
+                    h = psum_h.tile([P, BLOCK], F32)
+                    for g in range(PASSES1):
+                        nc.tensor.matmul_mx(
+                            out=h[:],
+                            lhsT=w2_codes[:, g, t * P : (t + 1) * P].bitcast(FP8X4),
+                            lhsT_scale=w2_scales[:, g, t * P : (t + 1) * P],
+                            rhs=codes[:, g * BLOCK : (g + 1) * BLOCK].bitcast(FP8X4),
+                            rhs_scale=scales[:, g * BLOCK : (g + 1) * BLOCK],
+                            start=(g == 0),
+                            stop=(g == PASSES1 - 1),
+                        )
+                    nc.scalar.activation(
+                        out=planes[:, t, :], in_=h[:], func=ACT.Relu, bias=bias[:, t : t + 1]
+                    )
+                planes_of[j] = planes
+
+            def regroup_en2(j):
+                grouped2 = work.tile([P, BLOCK, PACK], BF16, align_bytes=64)
+                regroup(nc, grouped2[:], planes_of[j][:])
+                grouped2_of[j] = grouped2
+
+            def quantise_en2(j):
+                nc.vector.quantize_mx(
+                    out=en2_codes[:, block_cols(j)].bitcast(FP8X4),
+                    scales=en2_scales[:, block_cols(j)],
+                    in_=grouped2_of[j][:].rearrange("p c t -> p (c t)"),
+                )
+
+            def take_statistics(j):
+                for i, product in enumerate(products_of[j]):
+                    nc.vector.bn_stats(out=stats[:, i, j, :], in_=product[:])
+
+            def prepare_weights():
+                regroup_w2 = prep.tile([P, PASSES1, K2, PACK], BF16, align_bytes=64)
+                for g in range(PASSES1):
+                    regroup(nc, regroup_w2[:, g], w2_rows[:, g])
+                regroup_head = prep.tile([P, 2, D, PACK], BF16, align_bytes=64)
+                for i in range(2):
+                    regroup(nc, regroup_head[:, i], head_rows[:, i])
+                nc.vector.quantize_mx(
+                    out=w2_codes[:].rearrange("p g c -> p (g c)").bitcast(FP8X4),
+                    scales=w2_scales[:].rearrange("p g c -> p (g c)"),
+                    in_=regroup_w2[:].rearrange("p g c t -> p (g c t)"),
+                )
+                nc.vector.quantize_mx(
+                    out=head_codes[:].bitcast(FP8X4),
+                    scales=head_scales[:],
+                    in_=regroup_head[:].rearrange("p i c t -> p (i c t)"),
+                )
+                b2_t = psum_t.tile([P, P], BF16, tag="xt")
+                nc.tensor.transpose(b2_t[:], b2_rows[:], ident_bf16[:])
+                nc.vector.tensor_copy(out=bias[:], in_=b2_t[:, 0:K2_TILES])
+
+            load_block(0)
+            w2_rows = prep.tile([P, PASSES1, PACK, K2], BF16)
+            nc.sync.dma_start(
+                out=w2_rows[:].rearrange("p g (u e) c -> p (g u) (e c)", e=2),
+                in_=W2.rearrange("(q p e) c -> p q (e c)", p=P, e=2),
+            )
+            load_block(1)
+            b2_rows = prep.tile([P, P], BF16)
+            nc.vector.memset(b2_rows[:], 0.0)
+            nc.sync.dma_start(
+                out=b2_rows[0:K2_TILES, :], in_=b2.rearrange("(t p) -> t p", p=P)
+            )
+            head_rows = prep.tile([P, 2, PACK, D], BF16)
+            for i, weight in enumerate((Wmean, Wlogvar)):
+                nc.sync.dma_start(
+                    out=head_rows[:, i], in_=weight.rearrange("(t p) d -> p t d", p=P)
+                )
+            load_block(2)
+
+            transpose_block(0)
+            prepare_weights()
+            quantise_en1(0)
+            for i in range(NBLOCKS + 3):
+                if i >= 3:
+                    take_statistics(i - 3)
+                if i + LOADS_AHEAD < NBLOCKS:
+                    load_block(i + LOADS_AHEAD)
+                if i + LOADS_AHEAD == NBLOCKS:
+                    nc.sync.dma_start(
+                        out=eps_rows[:].rearrange("r j s d -> r j (s d)"),
+                        in_=eps.rearrange("(j r s) d -> r j (s d)", r=P, s=SUB),
+                    )
+                if i + 1 < NBLOCKS:
+                    transpose_block(i + 1)
+                if 1 <= i <= NBLOCKS:
+                    regroup_en2(i - 1)
+                if i + 1 < NBLOCKS:
+                    quantise_en1(i + 1)
+                if 1 <= i <= NBLOCKS:
+                    quantise_en2(i - 1)
+                if i < NBLOCKS:
+                    first_product(i)
+                if 2 <= i <= NBLOCKS + 1:
+                    products_of[i - 2] = second_products(psum_s, i - 2)
+
+        with ExitStack() as phase:
+            small = phase.enter_context(tc.tile_pool(name="small", bufs=1))
+            work = phase.enter_context(tc.tile_pool(name="tail", bufs=3))
+            psum_e = phase.enter_context(tc.psum_pool(name="psum_e", bufs=2))
+            psum_p = phase.enter_context(tc.psum_pool(name="psum_p", bufs=2))
+            psum_b = phase.enter_context(tc.psum_pool(name="psum_b", bufs=2))
+
+            mean_var = small.tile([P, 2, 2], F32)
+            for i in range(2):
+                nc.vector.bn_aggr(
+                    out=mean_var[:, i, :], in_=stats[:, i].rearrange("p j v -> p (j v)")
+                )
+            rstd = reciprocal_std(nc, small, mean_var[:, :, 1], minus_half, "rstd")
+            shift = small.tile([P, 2], F32)
+            nc.vector.scalar_tensor_tensor(
+                out=shift[:], in0=mean_var[:, :, 0], scalar=-1.0, in1=rstd[:],
+                op0=ALU.mult, op1=ALU.mult,
+            )
+            half_rstd = small.tile([P, 1], F32)
+            nc.vector.tensor_scalar_mul(out=half_rstd[:], in0=rstd[:, 1:2], scalar1=0.5)
+            half_shift = small.tile([P, 1], F32)
+            nc.vector.tensor_scalar_mul(out=half_shift[:], in0=shift[:, 1:2], scalar1=0.5)
+            shift_ps = psum_b.tile([P, D], F32, tag="back")
+            nc.tensor.matmul(
+                out=shift_ps[:], lhsT=shift[:, 0:1].to_broadcast([P, P]), rhs=ident_f32[:],
+                start=True, stop=True,
+            )
+            shift_row = small.tile([P, D], F32)
+            nc.vector.tensor_copy(out=shift_row[:], in_=shift_ps[:])
+
+            z_less_shift = small.tile([P, ROWS], F32)
+            z_sums = small.tile([P, NBLOCKS], F32)
+            z_squares = small.tile([P, NBLOCKS], F32)
+
+            def sample_block(j):
+                eps_ps = psum_e.tile([P, SUB, P], BF16)
+                for s in range(SUB):
+                    nc.tensor.transpose(eps_ps[:, s, :], eps_rows[:, j, s, :], ident_bf16[:])
+                eps_t = work.tile([P, BLOCK], BF16)
+                nc.scalar.copy(out=eps_t[:], in_=eps_ps[:].rearrange("p s r -> p (s r)"))
+                m_ps, lv_ps = second_products(psum_p, j)
+                std = work.tile([P, BLOCK], F32)
+                nc.scalar.activation(
+                    out=std[:], in_=lv_ps[:], func=ACT.Exp, bias=half_shift[:], scale=half_rstd[:]
+                )
+                noise = work.tile([P, BLOCK], F32)
+                nc.vector.tensor_tensor(out=noise[:], in0=std[:], in1=eps_t[:], op=ALU.mult)
+                nc.vector.scalar_tensor_tensor(
+                    out=z_less_shift[:, block_cols(j)], in0=m_ps[:], scalar=rstd[:, 0:1],
+                    in1=noise[:], op0=ALU.mult, op1=ALU.add, accum_out=z_sums[:, j : j + 1],
+                )
+
+            def transpose_back(source):
+                back = psum_b.tile([P, SUB, D], F32, tag="back")
+                for s in range(SUB):
+                    nc.tensor.transpose(back[:, s, :], source[:, s * P : (s + 1) * P], ident_f32[:])
+                return back
+
+            def store_z(j):
+                squares = work.tile([P, BLOCK], F32)
+                nc.scalar.activation(
+                    out=squares[:], in_=z_less_shift[:, block_cols(j)], func=ACT.Square,
+                    bias=shift[:, 0:1], accum_out=z_squares[:, j : j + 1],
+                )
+                back = transpose_back(z_less_shift[:, block_cols(j)])
+                z_rows = work.tile([P, SUB, D], F32)
+                nc.vector.tensor_tensor(
+                    out=z_rows[:], in0=back[:],
+                    in1=shift_row[:].unsqueeze(1).to_broadcast([P, SUB, D]), op=ALU.add,
+                )
+                nc.sync.dma_start(
+                    out=block_rows(out_0, j), in_=z_rows[:].rearrange("r s d -> r (s d)")
+                )
+
+            for j in range(NBLOCKS + 1):
+                if j < NBLOCKS:
+                    sample_block(j)
+                if j >= 1:
+                    store_z(j - 1)
+
+            z_sum = small.tile([P, 1], F32)
+            nc.vector.tensor_reduce(out=z_sum[:], in_=z_sums[:], axis=AXIS.X, op=ALU.add)
+            z_square = small.tile([P, 1], F32)
+            nc.vector.tensor_reduce(out=z_square[:], in_=z_squares[:], axis=AXIS.X, op=ALU.add)
+            z_mean = small.tile([P, 1], F32)
+            nc.vector.tensor_scalar(
+                out=z_mean[:], in0=z_sum[:], scalar1=1.0 / ROWS, scalar2=shift[:, 0:1],
+                op0=ALU.mult, op1=ALU.add,
+            )
+            z_mean_squared = small.tile([P, 1], F32)
+            nc.vector.tensor_tensor(
+                out=z_mean_squared[:], in0=z_mean[:], in1=z_mean[:], op=ALU.mult
+            )
+            z_var = small.tile([P, 1], F32)
+            nc.vector.scalar_tensor_tensor(
+                out=z_var[:], in0=z_square[:], scalar=1.0 / ROWS, in1=z_mean_squared[:],
+                op0=ALU.mult, op1=ALU.subtract,
+            )
+            z_rstd = reciprocal_std(nc, small, z_var[:], minus_half, "z_rstd")
+            zx_shift = small.tile([P, 1], F32)
+            nc.vector.tensor_scalar(
+                out=zx_shift[:], in0=z_sum[:], scalar1=-1.0 / ROWS, scalar2=z_rstd[:],
+                op0=ALU.mult, op1=ALU.mult,
+            )
+
+            for j in range(NBLOCKS):
+                zx_t = work.tile([P, BLOCK], F32)
+                nc.vector.tensor_scalar(
+                    out=zx_t[:], in0=z_less_shift[:, block_cols(j)], scalar1=z_rstd[:],
+                    scalar2=zx_shift[:], op0=ALU.mult, op1=ALU.add,
+                )
+                back = transpose_back(zx_t[:])
+                zx_rows = work.tile([P, SUB * D], F32)
+                nc.scalar.copy(out=zx_rows[:], in_=back[:].rearrange("r s d -> r (s d)"))
+                nc.sync.dma_start(out=block_rows(out_1, j), in_=zx_rows[:])

@@ -23,10 +23,13 @@ BLOCK = 512
 NBLOCKS = ROWS // BLOCK
 SUB = BLOCK // P
 K2_TILES = K2 // P
-WORDS = K1 // 2
+PSUM_BANKS = 8
 BN_EPS = 1e-5
 BN_STATS_DIM = 6
 LOADS_AHEAD = 3
+DRAIN_STEPS = 4
+M = 0
+LV = 1
 
 FLOPS = 2 * ROWS * (K1 * K2 + K2 * 2 * D)
 
@@ -39,24 +42,11 @@ def block_rows(dram, j):
     return dram[j * BLOCK : (j + 1) * BLOCK, :].rearrange("(r s) w -> r (s w)", s=SUB)
 
 
-def regroup(nc, grouped, planes):
-    nc.vector.tensor_copy(
-        out=grouped.rearrange("p (c i) t -> p c t i", i=4),
-        in_=planes.rearrange("p t (c i) -> p c t i", i=4),
-    )
-
-
-def reciprocal_std(nc, pool, variance, minus_half, name):
-    shape = [P, variance.shape[1]]
-    padded = pool.tile(shape, F32, name=name + "_padded")
-    nc.gpsimd.tensor_scalar(
-        out=padded[:], in0=variance, scalar1=1.0, scalar2=BN_EPS, op0=ALU.mult, op1=ALU.add
-    )
-    rstd = pool.tile(shape, F32, name=name)
-    nc.gpsimd.tensor_tensor(
-        out=rstd[:], in0=padded[:], in1=minus_half[:, 0 : shape[1]], op=ALU.pow
-    )
-    return rstd
+def regrouped(grouped, planes):
+    return {
+        "out": grouped.rearrange("p (c i) t -> p c t i", i=4),
+        "in_": planes.rearrange("p t (c i) -> p c t i", i=4),
+    }
 
 
 def tile_modelvd_pa_t_kernel(tc, en1, W2, b2, Wmean, Wlogvar, eps, out_0, out_1):
@@ -64,6 +54,7 @@ def tile_modelvd_pa_t_kernel(tc, en1, W2, b2, Wmean, Wlogvar, eps, out_0, out_1)
     with ExitStack() as kernel_scope:
         kernel_scope.enter_context(tc.manual_schedule())
         keep = kernel_scope.enter_context(tc.tile_pool(name="keep", bufs=1))
+        psum = kernel_scope.enter_context(tc.psum_pool(name="psum", bufs=PSUM_BANKS))
 
         ident_f32 = keep.tile([P, P], F32)
         make_identity(nc, ident_f32[:])
@@ -71,6 +62,9 @@ def tile_modelvd_pa_t_kernel(tc, en1, W2, b2, Wmean, Wlogvar, eps, out_0, out_1)
         make_identity(nc, ident_bf16[:])
         minus_half = keep.tile([P, 2], F32)
         nc.gpsimd.memset(minus_half[:], -0.5)
+        one_four = keep.tile([P, 2], F32)
+        nc.gpsimd.memset(one_four[:, M : M + 1], 1.0)
+        nc.gpsimd.memset(one_four[:, LV : LV + 1], 4.0)
 
         warm = keep.tile([P, 1], F32)
         nc.vector.memset(warm[:], 0.0)
@@ -78,37 +72,31 @@ def tile_modelvd_pa_t_kernel(tc, en1, W2, b2, Wmean, Wlogvar, eps, out_0, out_1)
 
         w2_codes = keep.tile([P, PASSES1, K2], U32, align_bytes=64)
         w2_scales = keep.tile([P, PASSES1, K2], U8, align_bytes=64)
-        head_codes = keep.tile([P, 2 * D], U32, align_bytes=64)
-        head_scales = keep.tile([P, 2 * D], U8, align_bytes=64)
+        head_codes = keep.tile([P, 2, D], U32, align_bytes=64)
+        head_scales = keep.tile([P, 2, D], U8, align_bytes=64)
         bias = keep.tile([P, K2_TILES], F32)
         en2_codes = keep.tile([P, ROWS], U32, align_bytes=64)
         en2_scales = keep.tile([P, ROWS], U8, align_bytes=64)
-        eps_rows = keep.tile([P, NBLOCKS, SUB, D], BF16)
+        eps_t = keep.tile([P, ROWS], BF16)
         stats = keep.tile([P, 2, NBLOCKS, BN_STATS_DIM], F32)
 
-        def second_products(psum, j):
-            products = []
-            for i, name in enumerate(("m_ps", "lv_ps")):
-                product = psum.tile([P, BLOCK], F32, name=name)
-                nc.tensor.matmul_mx(
-                    out=product[:],
-                    lhsT=head_codes[:, i * D : (i + 1) * D].bitcast(FP8X4),
-                    lhsT_scale=head_scales[:, i * D : (i + 1) * D],
-                    rhs=en2_codes[:, block_cols(j)].bitcast(FP8X4),
-                    rhs_scale=en2_scales[:, block_cols(j)],
-                    start=True,
-                    stop=True,
-                )
-                products.append(product)
-            return products
+        def head_product(i, j):
+            product = psum.tile([P, BLOCK], F32, tag="bank")
+            nc.tensor.matmul_mx(
+                out=product[:],
+                lhsT=head_codes[:, i, :].bitcast(FP8X4),
+                lhsT_scale=head_scales[:, i, :],
+                rhs=en2_codes[:, block_cols(j)].bitcast(FP8X4),
+                rhs_scale=en2_scales[:, block_cols(j)],
+                start=True,
+                stop=True,
+            )
+            return product
 
         with ExitStack() as phase:
             prep = phase.enter_context(tc.tile_pool(name="prep", bufs=1))
             loads = phase.enter_context(tc.tile_pool(name="loads", bufs=LOADS_AHEAD + 1))
             work = phase.enter_context(tc.tile_pool(name="work", bufs=2))
-            psum_t = phase.enter_context(tc.psum_pool(name="psum_t", bufs=3))
-            psum_h = phase.enter_context(tc.psum_pool(name="psum_h", bufs=3))
-            psum_s = phase.enter_context(tc.psum_pool(name="psum_s", bufs=1))
 
             x_of = {}
             grouped1_of = {}
@@ -130,7 +118,7 @@ def tile_modelvd_pa_t_kernel(tc, en1, W2, b2, Wmean, Wlogvar, eps, out_0, out_1)
                 )
                 for b in range(2 * PASSES1):
                     g, half = divmod(b, 2)
-                    xt = psum_t.tile([P, 2, 2, P], F32, tag="xt")
+                    xt = psum.tile([P, 2, 2, P], F32, tag="bank")
                     for s in range(2):
                         for u in range(2):
                             first = (2 * g + u) * P
@@ -158,7 +146,7 @@ def tile_modelvd_pa_t_kernel(tc, en1, W2, b2, Wmean, Wlogvar, eps, out_0, out_1)
                 codes, scales = en1_mx_of[j]
                 planes = work.tile([P, K2_TILES, BLOCK], BF16)
                 for t in range(K2_TILES):
-                    h = psum_h.tile([P, BLOCK], F32)
+                    h = psum.tile([P, BLOCK], F32, tag="bank")
                     for g in range(PASSES1):
                         nc.tensor.matmul_mx(
                             out=h[:],
@@ -176,7 +164,7 @@ def tile_modelvd_pa_t_kernel(tc, en1, W2, b2, Wmean, Wlogvar, eps, out_0, out_1)
 
             def regroup_en2(j):
                 grouped2 = work.tile([P, BLOCK, PACK], BF16, align_bytes=64)
-                regroup(nc, grouped2[:], planes_of[j][:])
+                nc.vector.tensor_copy(**regrouped(grouped2[:], planes_of[j][:]))
                 grouped2_of[j] = grouped2
 
             def quantise_en2(j):
@@ -187,52 +175,69 @@ def tile_modelvd_pa_t_kernel(tc, en1, W2, b2, Wmean, Wlogvar, eps, out_0, out_1)
                 )
 
             def take_statistics(j):
-                for i, product in enumerate(products_of[j]):
-                    nc.vector.bn_stats(out=stats[:, i, j, :], in_=product[:])
+                for i in (M, LV):
+                    nc.vector.bn_stats(out=stats[:, i, j, :], in_=products_of[j][i][:])
 
-            def prepare_weights():
-                regroup_w2 = prep.tile([P, PASSES1, K2, PACK], BF16, align_bytes=64)
+            def transpose_eps(first_block, blocks):
+                for j in range(first_block, first_block + blocks, 2):
+                    eps_ps = psum.tile([P, 2 * SUB, P], BF16, tag="bank")
+                    for c in range(2 * SUB):
+                        nc.tensor.transpose(
+                            eps_ps[:, c, :], eps_rows[:, j * SUB + c, :], ident_bf16[:]
+                        )
+                    nc.scalar.copy(
+                        out=eps_t[:, j * BLOCK : (j + 2) * BLOCK],
+                        in_=eps_ps[:].rearrange("p c r -> p (c r)"),
+                    )
+
+            def prepare_w2():
+                w2_grouped = prep.tile([P, PASSES1, K2, PACK], BF16, align_bytes=64)
+                nc.vector.tensor_copy(**regrouped(w2_grouped[:, 0], w2_rows[:, 0]))
+                nc.scalar.copy(**regrouped(w2_grouped[:, 1], w2_rows[:, 1]))
                 for g in range(PASSES1):
-                    regroup(nc, regroup_w2[:, g], w2_rows[:, g])
-                regroup_head = prep.tile([P, 2, D, PACK], BF16, align_bytes=64)
-                for i in range(2):
-                    regroup(nc, regroup_head[:, i], head_rows[:, i])
-                nc.vector.quantize_mx(
-                    out=w2_codes[:].rearrange("p g c -> p (g c)").bitcast(FP8X4),
-                    scales=w2_scales[:].rearrange("p g c -> p (g c)"),
-                    in_=regroup_w2[:].rearrange("p g c t -> p (g c t)"),
-                )
-                nc.vector.quantize_mx(
-                    out=head_codes[:].bitcast(FP8X4),
-                    scales=head_scales[:],
-                    in_=regroup_head[:].rearrange("p i c t -> p (i c t)"),
-                )
-                b2_t = psum_t.tile([P, P], BF16, tag="xt")
+                    nc.vector.quantize_mx(
+                        out=w2_codes[:, g, :].bitcast(FP8X4),
+                        scales=w2_scales[:, g, :],
+                        in_=w2_grouped[:, g].rearrange("p c t -> p (c t)"),
+                    )
+
+            def prepare_bias_and_heads():
+                b2_t = psum.tile([P, P], BF16, tag="bank")
                 nc.tensor.transpose(b2_t[:], b2_rows[:], ident_bf16[:])
                 nc.vector.tensor_copy(out=bias[:], in_=b2_t[:, 0:K2_TILES])
+                head_grouped = prep.tile([P, 2, D, PACK], BF16, align_bytes=64)
+                for i in (M, LV):
+                    nc.vector.tensor_copy(**regrouped(head_grouped[:, i], head_rows[:, i]))
+                nc.vector.quantize_mx(
+                    out=head_codes[:].rearrange("p i d -> p (i d)").bitcast(FP8X4),
+                    scales=head_scales[:].rearrange("p i d -> p (i d)"),
+                    in_=head_grouped[:].rearrange("p i d t -> p (i d t)"),
+                )
 
-            load_block(0)
             w2_rows = prep.tile([P, PASSES1, PACK, K2], BF16)
             nc.sync.dma_start(
                 out=w2_rows[:].rearrange("p g (u e) c -> p (g u) (e c)", e=2),
                 in_=W2.rearrange("(q p e) c -> p q (e c)", p=P, e=2),
             )
-            load_block(1)
+            load_block(0)
             b2_rows = prep.tile([P, P], BF16)
             nc.vector.memset(b2_rows[:], 0.0)
             nc.sync.dma_start(
                 out=b2_rows[0:K2_TILES, :], in_=b2.rearrange("(t p) -> t p", p=P)
             )
             head_rows = prep.tile([P, 2, PACK, D], BF16)
-            for i, weight in enumerate((Wmean, Wlogvar)):
+            for i, weight in ((M, Wmean), (LV, Wlogvar)):
                 nc.sync.dma_start(
                     out=head_rows[:, i], in_=weight.rearrange("(t p) d -> p t d", p=P)
                 )
+            load_block(1)
             load_block(2)
+            eps_rows = prep.tile([P, NBLOCKS * SUB, D], BF16)
 
+            prepare_w2()
             transpose_block(0)
-            prepare_weights()
             quantise_en1(0)
+            prepare_bias_and_heads()
             for i in range(NBLOCKS + 3):
                 if i >= 3:
                     take_statistics(i - 3)
@@ -240,7 +245,7 @@ def tile_modelvd_pa_t_kernel(tc, en1, W2, b2, Wmean, Wlogvar, eps, out_0, out_1)
                     load_block(i + LOADS_AHEAD)
                 if i + LOADS_AHEAD == NBLOCKS:
                     nc.sync.dma_start(
-                        out=eps_rows[:].rearrange("r j s d -> r j (s d)"),
+                        out=eps_rows[:].rearrange("r (j s) d -> r j (s d)", s=SUB),
                         in_=eps.rearrange("(j r s) d -> r j (s d)", r=P, s=SUB),
                     )
                 if i + 1 < NBLOCKS:
@@ -254,74 +259,87 @@ def tile_modelvd_pa_t_kernel(tc, en1, W2, b2, Wmean, Wlogvar, eps, out_0, out_1)
                 if i < NBLOCKS:
                     first_product(i)
                 if 2 <= i <= NBLOCKS + 1:
-                    products_of[i - 2] = second_products(psum_s, i - 2)
+                    products_of[i - 2] = (head_product(M, i - 2), head_product(LV, i - 2))
+                if i >= NBLOCKS + 3 - DRAIN_STEPS:
+                    share = NBLOCKS // DRAIN_STEPS
+                    transpose_eps((i - (NBLOCKS + 3 - DRAIN_STEPS)) * share, share)
 
         with ExitStack() as phase:
             small = phase.enter_context(tc.tile_pool(name="small", bufs=1))
-            work = phase.enter_context(tc.tile_pool(name="tail", bufs=3))
-            psum_e = phase.enter_context(tc.psum_pool(name="psum_e", bufs=2))
-            psum_p = phase.enter_context(tc.psum_pool(name="psum_p", bufs=2))
-            psum_b = phase.enter_context(tc.psum_pool(name="psum_b", bufs=2))
+            tail = phase.enter_context(tc.tile_pool(name="tail", bufs=4))
+            staging = phase.enter_context(tc.tile_pool(name="staging", bufs=6))
+
+            lv_of = {0: head_product(LV, 0)}
+            m_of = {}
+            std_of = {}
+            noise_of = {}
 
             mean_var = small.tile([P, 2, 2], F32)
-            for i in range(2):
+            for i in (LV, M):
                 nc.vector.bn_aggr(
                     out=mean_var[:, i, :], in_=stats[:, i].rearrange("p j v -> p (j v)")
                 )
-            rstd = reciprocal_std(nc, small, mean_var[:, :, 1], minus_half, "rstd")
+            padded = small.tile([P, 2], F32)
+            nc.vector.scalar_tensor_tensor(
+                out=padded[:], in0=mean_var[:, :, 1], scalar=BN_EPS, in1=one_four[:],
+                op0=ALU.add, op1=ALU.mult,
+            )
+            factor = small.tile([P, 2], F32)
+            nc.gpsimd.tensor_tensor(out=factor[:], in0=padded[:], in1=minus_half[:], op=ALU.pow)
             shift = small.tile([P, 2], F32)
             nc.vector.scalar_tensor_tensor(
-                out=shift[:], in0=mean_var[:, :, 0], scalar=-1.0, in1=rstd[:],
+                out=shift[:], in0=mean_var[:, :, 0], scalar=-1.0, in1=factor[:],
                 op0=ALU.mult, op1=ALU.mult,
             )
-            half_rstd = small.tile([P, 1], F32)
-            nc.vector.tensor_scalar_mul(out=half_rstd[:], in0=rstd[:, 1:2], scalar1=0.5)
-            half_shift = small.tile([P, 1], F32)
-            nc.vector.tensor_scalar_mul(out=half_shift[:], in0=shift[:, 1:2], scalar1=0.5)
-            shift_ps = psum_b.tile([P, D], F32, tag="back")
+            shift_ps = psum.tile([P, D], F32, tag="bank")
             nc.tensor.matmul(
-                out=shift_ps[:], lhsT=shift[:, 0:1].to_broadcast([P, P]), rhs=ident_f32[:],
+                out=shift_ps[:], lhsT=shift[:, M : M + 1].to_broadcast([P, P]), rhs=ident_f32[:],
                 start=True, stop=True,
             )
             shift_row = small.tile([P, D], F32)
             nc.vector.tensor_copy(out=shift_row[:], in_=shift_ps[:])
 
             z_less_shift = small.tile([P, ROWS], F32)
-            z_sums = small.tile([P, NBLOCKS], F32)
-            z_squares = small.tile([P, NBLOCKS], F32)
+            z_sums = small.tile([P, 2, NBLOCKS], F32)
+
+            def std_block(j):
+                std = tail.tile([P, BLOCK], F32)
+                nc.scalar.activation(
+                    out=std[:], in_=lv_of[j][:], func=ACT.Exp,
+                    bias=shift[:, LV : LV + 1], scale=factor[:, LV : LV + 1],
+                )
+                std_of[j] = std
+
+            def noise_block(j):
+                noise = tail.tile([P, BLOCK], F32)
+                nc.gpsimd.tensor_tensor(
+                    out=noise[:], in0=std_of[j][:], in1=eps_t[:, block_cols(j)], op=ALU.mult
+                )
+                noise_of[j] = noise
 
             def sample_block(j):
-                eps_ps = psum_e.tile([P, SUB, P], BF16)
-                for s in range(SUB):
-                    nc.tensor.transpose(eps_ps[:, s, :], eps_rows[:, j, s, :], ident_bf16[:])
-                eps_t = work.tile([P, BLOCK], BF16)
-                nc.scalar.copy(out=eps_t[:], in_=eps_ps[:].rearrange("p s r -> p (s r)"))
-                m_ps, lv_ps = second_products(psum_p, j)
-                std = work.tile([P, BLOCK], F32)
-                nc.scalar.activation(
-                    out=std[:], in_=lv_ps[:], func=ACT.Exp, bias=half_shift[:], scale=half_rstd[:]
-                )
-                noise = work.tile([P, BLOCK], F32)
-                nc.vector.tensor_tensor(out=noise[:], in0=std[:], in1=eps_t[:], op=ALU.mult)
                 nc.vector.scalar_tensor_tensor(
-                    out=z_less_shift[:, block_cols(j)], in0=m_ps[:], scalar=rstd[:, 0:1],
-                    in1=noise[:], op0=ALU.mult, op1=ALU.add, accum_out=z_sums[:, j : j + 1],
+                    out=z_less_shift[:, block_cols(j)], in0=m_of[j][:],
+                    scalar=factor[:, M : M + 1], in1=noise_of[j][:],
+                    op0=ALU.mult, op1=ALU.add, accum_out=z_sums[:, 0, j : j + 1],
+                )
+
+            def square_block(j):
+                squares = tail.tile([P, BLOCK], F32)
+                nc.scalar.activation(
+                    out=squares[:], in_=z_less_shift[:, block_cols(j)], func=ACT.Square,
+                    bias=shift[:, M : M + 1], accum_out=z_sums[:, 1, j : j + 1],
                 )
 
             def transpose_back(source):
-                back = psum_b.tile([P, SUB, D], F32, tag="back")
+                back = psum.tile([P, SUB, D], F32, tag="bank")
                 for s in range(SUB):
                     nc.tensor.transpose(back[:, s, :], source[:, s * P : (s + 1) * P], ident_f32[:])
                 return back
 
             def store_z(j):
-                squares = work.tile([P, BLOCK], F32)
-                nc.scalar.activation(
-                    out=squares[:], in_=z_less_shift[:, block_cols(j)], func=ACT.Square,
-                    bias=shift[:, 0:1], accum_out=z_squares[:, j : j + 1],
-                )
                 back = transpose_back(z_less_shift[:, block_cols(j)])
-                z_rows = work.tile([P, SUB, D], F32)
+                z_rows = staging.tile([P, SUB, D], F32)
                 nc.vector.tensor_tensor(
                     out=z_rows[:], in0=back[:],
                     in1=shift_row[:].unsqueeze(1).to_broadcast([P, SUB, D]), op=ALU.add,
@@ -330,44 +348,55 @@ def tile_modelvd_pa_t_kernel(tc, en1, W2, b2, Wmean, Wlogvar, eps, out_0, out_1)
                     out=block_rows(out_0, j), in_=z_rows[:].rearrange("r s d -> r (s d)")
                 )
 
-            for j in range(NBLOCKS + 1):
+            for j in range(NBLOCKS + 4):
+                if j + 1 < NBLOCKS:
+                    lv_of[j + 1] = head_product(LV, j + 1)
+                if 1 <= j <= NBLOCKS:
+                    m_of[j - 1] = head_product(M, j - 1)
                 if j < NBLOCKS:
-                    sample_block(j)
-                if j >= 1:
-                    store_z(j - 1)
+                    std_block(j)
+                if 1 <= j <= NBLOCKS:
+                    noise_block(j - 1)
+                if 2 <= j <= NBLOCKS + 1:
+                    sample_block(j - 2)
+                if j >= 4:
+                    square_block(j - 4)
+                    store_z(j - 4)
 
-            z_sum = small.tile([P, 1], F32)
+            z_sum = small.tile([P, 2], F32)
             nc.vector.tensor_reduce(out=z_sum[:], in_=z_sums[:], axis=AXIS.X, op=ALU.add)
-            z_square = small.tile([P, 1], F32)
-            nc.vector.tensor_reduce(out=z_square[:], in_=z_squares[:], axis=AXIS.X, op=ALU.add)
             z_mean = small.tile([P, 1], F32)
             nc.vector.tensor_scalar(
-                out=z_mean[:], in0=z_sum[:], scalar1=1.0 / ROWS, scalar2=shift[:, 0:1],
+                out=z_mean[:], in0=z_sum[:, 0:1], scalar1=1.0 / ROWS, scalar2=shift[:, M : M + 1],
                 op0=ALU.mult, op1=ALU.add,
             )
-            z_mean_squared = small.tile([P, 1], F32)
-            nc.vector.tensor_tensor(
-                out=z_mean_squared[:], in0=z_mean[:], in1=z_mean[:], op=ALU.mult
-            )
-            z_var = small.tile([P, 1], F32)
-            nc.vector.scalar_tensor_tensor(
-                out=z_var[:], in0=z_square[:], scalar=1.0 / ROWS, in1=z_mean_squared[:],
+            z_mean2_less_eps = small.tile([P, 1], F32)
+            nc.vector.tensor_scalar(
+                out=z_mean2_less_eps[:], in0=z_mean[:], scalar1=z_mean[:], scalar2=BN_EPS,
                 op0=ALU.mult, op1=ALU.subtract,
             )
-            z_rstd = reciprocal_std(nc, small, z_var[:], minus_half, "z_rstd")
+            z_padded = small.tile([P, 1], F32)
+            nc.vector.tensor_scalar(
+                out=z_padded[:], in0=z_sum[:, 1:2], scalar1=1.0 / ROWS,
+                scalar2=z_mean2_less_eps[:], op0=ALU.mult, op1=ALU.subtract,
+            )
+            z_factor = small.tile([P, 1], F32)
+            nc.gpsimd.tensor_tensor(
+                out=z_factor[:], in0=z_padded[:], in1=minus_half[:, 0:1], op=ALU.pow
+            )
             zx_shift = small.tile([P, 1], F32)
             nc.vector.tensor_scalar(
-                out=zx_shift[:], in0=z_sum[:], scalar1=-1.0 / ROWS, scalar2=z_rstd[:],
+                out=zx_shift[:], in0=z_sum[:, 0:1], scalar1=-1.0 / ROWS, scalar2=z_factor[:],
                 op0=ALU.mult, op1=ALU.mult,
             )
 
             for j in range(NBLOCKS):
-                zx_t = work.tile([P, BLOCK], F32)
+                zx_t = tail.tile([P, BLOCK], F32)
                 nc.vector.tensor_scalar(
-                    out=zx_t[:], in0=z_less_shift[:, block_cols(j)], scalar1=z_rstd[:],
+                    out=zx_t[:], in0=z_less_shift[:, block_cols(j)], scalar1=z_factor[:],
                     scalar2=zx_shift[:], op0=ALU.mult, op1=ALU.add,
                 )
                 back = transpose_back(zx_t[:])
-                zx_rows = work.tile([P, SUB * D], F32)
+                zx_rows = staging.tile([P, SUB * D], F32)
                 nc.scalar.copy(out=zx_rows[:], in_=back[:].rearrange("r s d -> r (s d)"))
                 nc.sync.dma_start(out=block_rows(out_1, j), in_=zx_rows[:])

@@ -128,7 +128,7 @@ def tile_modelvd_pa_t_kernel(tc, en1, W2, b2, Wmean, Wlogvar, eps, out_0, out_1)
                                 ident_f32[:],
                             )
                     permuted = xt[:].rearrange("p s u r -> p s r u")
-                    if b == 2:
+                    if b == 2 and j % 2 == 0:
                         nc.vector.tensor_copy(out=pairs[:, b], in_=permuted)
                     else:
                         nc.scalar.copy(out=pairs[:, b], in_=permuted)

from contextlib import ExitStack

import concourse.mybir as mybir
from concourse.masks import make_identity

F32 = mybir.dt.float32
BF16 = mybir.dt.bfloat16
U32 = mybir.dt.uint32
U8 = mybir.dt.uint8
FP8X4 = mybir.dt.float8_e4m3fn_x4
ACT = mybir.ActivationFunctionType
ALU = mybir.AluOpType
AXIS = mybir.AxisListType

P = 128
PACK = 4
ROWS = 8192
K1 = 1024
K2 = 512
D = 128
PASSES1 = K1 // (P * PACK)
BLOCK = 512
NBLOCKS = ROWS // BLOCK
SUB = BLOCK // P
K2_TILES = K2 // P
PSUM_BANKS = 8
BN_EPS = 1e-5
BN_STATS_DIM = 6
LOADS_AHEAD = 3
DRAIN_STEPS = 4
M = 0
LV = 1

FLOPS = 2 * ROWS * (K1 * K2 + K2 * 2 * D)


def block_cols(j):
    return slice(j * BLOCK, (j + 1) * BLOCK)


def block_rows(dram, j):
    return dram[j * BLOCK : (j + 1) * BLOCK, :].rearrange("(r s) w -> r (s w)", s=SUB)


def regrouped(grouped, planes):
    return {
        "out": grouped.rearrange("p (c i) t -> p c t i", i=4),
        "in_": planes.rearrange("p t (c i) -> p c t i", i=4),
    }


def tile_modelvd_pa_t_kernel(tc, en1, W2, b2, Wmean, Wlogvar, eps, out_0, out_1):
    nc = tc.nc
    with ExitStack() as kernel_scope:
        kernel_scope.enter_context(tc.manual_schedule())
        keep = kernel_scope.enter_context(tc.tile_pool(name="keep", bufs=1))
        psum = kernel_scope.enter_context(tc.psum_pool(name="psum", bufs=PSUM_BANKS))

        ident_f32 = keep.tile([P, P], F32)
        make_identity(nc, ident_f32[:])
        ident_bf16 = keep.tile([P, P], BF16)
        make_identity(nc, ident_bf16[:])
        minus_half = keep.tile([P, 2], F32)
        nc.gpsimd.memset(minus_half[:], -0.5)
        one_four = keep.tile([P, 2], F32)
        nc.gpsimd.memset(one_four[:, M : M + 1], 1.0)
        nc.gpsimd.memset(one_four[:, LV : LV + 1], 4.0)

        warm = keep.tile([P, 1], F32)
        nc.vector.memset(warm[:], 0.0)
        nc.scalar.activation(out=warm[:], in_=warm[:], func=ACT.Exp)

        w2_codes = keep.tile([P, PASSES1, K2], U32, align_bytes=64)
        w2_scales = keep.tile([P, PASSES1, K2], U8, align_bytes=64)
        head_codes = keep.tile([P, 2, D], U32, align_bytes=64)
        head_scales = keep.tile([P, 2, D], U8, align_bytes=64)
        bias = keep.tile([P, K2_TILES], F32)
        en2_codes = keep.tile([P, ROWS], U32, align_bytes=64)
        en2_scales = keep.tile([P, ROWS], U8, align_bytes=64)
        eps_t = keep.tile([P, ROWS], BF16)
        stats = keep.tile([P, 2, NBLOCKS, BN_STATS_DIM], F32)

        def head_product(i, j):
            product = psum.tile([P, BLOCK], F32, tag="bank")
            nc.tensor.matmul_mx(
                out=product[:],
                lhsT=head_codes[:, i, :].bitcast(FP8X4),
                lhsT_scale=head_scales[:, i, :],
                rhs=en2_codes[:, block_cols(j)].bitcast(FP8X4),
                rhs_scale=en2_scales[:, block_cols(j)],
                start=True,
                stop=True,
            )
            return product

        with ExitStack() as phase:
            prep = phase.enter_context(tc.tile_pool(name="prep", bufs=1))
            loads = phase.enter_context(tc.tile_pool(name="loads", bufs=LOADS_AHEAD + 1))
            work = phase.enter_context(tc.tile_pool(name="work", bufs=2))

            x_of = {}
            grouped1_of = {}
            en1_mx_of = {}
            planes_of = {}
            grouped2_of = {}
            products_of = {}

            def load_block(j):
                x = loads.tile([P, SUB * K1], BF16, name="x")
                nc.sync.dma_start(out=x[:], in_=block_rows(en1, j))
                x_of[j] = x

            def transpose_block(j):
                words = x_of[j][:].bitcast(F32).rearrange("p (s w) -> p s w", s=SUB)
                grouped1 = work.tile([P, PASSES1 * BLOCK * PACK], BF16, align_bytes=64)
                pairs = grouped1[:].bitcast(F32).rearrange(
                    "p (b s r u) -> p b s r u", b=2 * PASSES1, s=2, r=P, u=2
                )
                for b in range(2 * PASSES1):
                    g, half = divmod(b, 2)
                    xt = psum.tile([P, 2, 2, P], F32, tag="bank")
                    for s in range(2):
                        for u in range(2):
                            first = (2 * g + u) * P
                            nc.tensor.transpose(
                                xt[:, s, u, :],
                                words[:, 2 * half + s, first : first + P],
                                ident_f32[:],
                            )
                    permuted = xt[:].rearrange("p s u r -> p s r u")
                    if b == 2 and j % 2 == 0:
                        nc.vector.tensor_copy(out=pairs[:, b], in_=permuted)
                    else:
                        nc.scalar.copy(out=pairs[:, b], in_=permuted)
                grouped1_of[j] = grouped1

            def quantise_en1(j):
                codes = work.tile([P, PASSES1 * BLOCK], U32, name="en1_codes", align_bytes=64)
                scales = work.tile([P, PASSES1 * BLOCK], U8, name="en1_scales", align_bytes=64)
                nc.vector.quantize_mx(
                    out=codes[:].bitcast(FP8X4), scales=scales[:], in_=grouped1_of[j][:]
                )
                en1_mx_of[j] = (codes, scales)

            def first_product(j):
                codes, scales = en1_mx_of[j]
                planes = work.tile([P, K2_TILES, BLOCK], BF16)
                for t in range(K2_TILES):
                    h = psum.tile([P, BLOCK], F32, tag="bank")
                    for g in range(PASSES1):
                        nc.tensor.matmul_mx(
                            out=h[:],
                            lhsT=w2_codes[:, g, t * P : (t + 1) * P].bitcast(FP8X4),
                            lhsT_scale=w2_scales[:, g, t * P : (t + 1) * P],
                            rhs=codes[:, g * BLOCK : (g + 1) * BLOCK].bitcast(FP8X4),
                            rhs_scale=scales[:, g * BLOCK : (g + 1) * BLOCK],
                            start=(g == 0),
                            stop=(g == PASSES1 - 1),
                        )
                    nc.scalar.activation(
                        out=planes[:, t, :], in_=h[:], func=ACT.Relu, bias=bias[:, t : t + 1]
                    )
                planes_of[j] = planes

            def regroup_en2(j):
                grouped2 = work.tile([P, BLOCK, PACK], BF16, align_bytes=64)
                nc.vector.tensor_copy(**regrouped(grouped2[:], planes_of[j][:]))
                grouped2_of[j] = grouped2

            def quantise_en2(j):
                nc.vector.quantize_mx(
                    out=en2_codes[:, block_cols(j)].bitcast(FP8X4),
                    scales=en2_scales[:, block_cols(j)],
                    in_=grouped2_of[j][:].rearrange("p c t -> p (c t)"),
                )

            def take_statistics(j):
                for i in (M, LV):
                    nc.vector.bn_stats(out=stats[:, i, j, :], in_=products_of[j][i][:])

            def transpose_eps(first_block, blocks):
                for j in range(first_block, first_block + blocks, 2):
                    eps_ps = psum.tile([P, 2 * SUB, P], BF16, tag="bank")
                    for c in range(2 * SUB):
                        nc.tensor.transpose(
                            eps_ps[:, c, :], eps_rows[:, j * SUB + c, :], ident_bf16[:]
                        )
                    nc.scalar.copy(
                        out=eps_t[:, j * BLOCK : (j + 2) * BLOCK],
                        in_=eps_ps[:].rearrange("p c r -> p (c r)"),
                    )

            def prepare_w2():
                w2_grouped = prep.tile([P, PASSES1, K2, PACK], BF16, align_bytes=64)
                nc.vector.tensor_copy(**regrouped(w2_grouped[:, 0], w2_rows[:, 0]))
                nc.scalar.copy(**regrouped(w2_grouped[:, 1], w2_rows[:, 1]))
                for g in range(PASSES1):
                    nc.vector.quantize_mx(
                        out=w2_codes[:, g, :].bitcast(FP8X4),
                        scales=w2_scales[:, g, :],
                        in_=w2_grouped[:, g].rearrange("p c t -> p (c t)"),
                    )

            def prepare_bias_and_heads():
                b2_t = psum.tile([P, P], BF16, tag="bank")
                nc.tensor.transpose(b2_t[:], b2_rows[:], ident_bf16[:])
                nc.vector.tensor_copy(out=bias[:], in_=b2_t[:, 0:K2_TILES])
                head_grouped = prep.tile([P, 2, D, PACK], BF16, align_bytes=64)
                for i in (M, LV):
                    nc.vector.tensor_copy(**regrouped(head_grouped[:, i], head_rows[:, i]))
                nc.vector.quantize_mx(
                    out=head_codes[:].rearrange("p i d -> p (i d)").bitcast(FP8X4),
                    scales=head_scales[:].rearrange("p i d -> p (i d)"),
                    in_=head_grouped[:].rearrange("p i d t -> p (i d t)"),
                )

            w2_rows = prep.tile([P, PASSES1, PACK, K2], BF16)
            nc.sync.dma_start(
                out=w2_rows[:].rearrange("p g (u e) c -> p (g u) (e c)", e=2),
                in_=W2.rearrange("(q p e) c -> p q (e c)", p=P, e=2),
            )
            load_block(0)
            b2_rows = prep.tile([P, P], BF16)
            nc.vector.memset(b2_rows[:], 0.0)
            nc.sync.dma_start(
                out=b2_rows[0:K2_TILES, :], in_=b2.rearrange("(t p) -> t p", p=P)
            )
            head_rows = prep.tile([P, 2, PACK, D], BF16)
            for i, weight in ((M, Wmean), (LV, Wlogvar)):
                nc.sync.dma_start(
                    out=head_rows[:, i], in_=weight.rearrange("(t p) d -> p t d", p=P)
                )
            load_block(1)
            load_block(2)
            eps_rows = prep.tile([P, NBLOCKS * SUB, D], BF16)

            prepare_w2()
            transpose_block(0)
            quantise_en1(0)
            prepare_bias_and_heads()
            for i in range(NBLOCKS + 3):
                if i >= 3:
                    take_statistics(i - 3)
                if i + LOADS_AHEAD < NBLOCKS:
                    load_block(i + LOADS_AHEAD)
                if i + LOADS_AHEAD == NBLOCKS:
                    nc.sync.dma_start(
                        out=eps_rows[:].rearrange("r (j s) d -> r j (s d)", s=SUB),
                        in_=eps.rearrange("(j r s) d -> r j (s d)", r=P, s=SUB),
                    )
                if i + 1 < NBLOCKS:
                    transpose_block(i + 1)
                if 1 <= i <= NBLOCKS:
                    regroup_en2(i - 1)
                if i + 1 < NBLOCKS:
                    quantise_en1(i + 1)
                if 1 <= i <= NBLOCKS:
                    quantise_en2(i - 1)
                if i < NBLOCKS:
                    first_product(i)
                if 2 <= i <= NBLOCKS + 1:
                    products_of[i - 2] = (head_product(M, i - 2), head_product(LV, i - 2))
                if i >= NBLOCKS + 3 - DRAIN_STEPS:
                    share = NBLOCKS // DRAIN_STEPS
                    transpose_eps((i - (NBLOCKS + 3 - DRAIN_STEPS)) * share, share)

        with ExitStack() as phase:
            small = phase.enter_context(tc.tile_pool(name="small", bufs=1))
            tail = phase.enter_context(tc.tile_pool(name="tail", bufs=4))
            staging = phase.enter_context(tc.tile_pool(name="staging", bufs=6))

            lv_of = {0: head_product(LV, 0)}
            m_of = {}
            std_of = {}
            noise_of = {}

            mean_var = small.tile([P, 2, 2], F32)
            for i in (LV, M):
                nc.vector.bn_aggr(
                    out=mean_var[:, i, :], in_=stats[:, i].rearrange("p j v -> p (j v)")
                )
            padded = small.tile([P, 2], F32)
            nc.vector.scalar_tensor_tensor(
                out=padded[:], in0=mean_var[:, :, 1], scalar=BN_EPS, in1=one_four[:],
                op0=ALU.add, op1=ALU.mult,
            )
            factor = small.tile([P, 2], F32)
            nc.gpsimd.tensor_tensor(out=factor[:], in0=padded[:], in1=minus_half[:], op=ALU.pow)
            shift = small.tile([P, 2], F32)
            nc.vector.scalar_tensor_tensor(
                out=shift[:], in0=mean_var[:, :, 0], scalar=-1.0, in1=factor[:],
                op0=ALU.mult, op1=ALU.mult,
            )
            shift_ps = psum.tile([P, D], F32, tag="bank")
            nc.tensor.matmul(
                out=shift_ps[:], lhsT=shift[:, M : M + 1].to_broadcast([P, P]), rhs=ident_f32[:],
                start=True, stop=True,
            )
            shift_row = small.tile([P, D], F32)
            nc.vector.tensor_copy(out=shift_row[:], in_=shift_ps[:])

            z_less_shift = small.tile([P, ROWS], F32)
            z_sums = small.tile([P, 2, NBLOCKS], F32)

            def std_block(j):
                std = tail.tile([P, BLOCK], F32)
                nc.scalar.activation(
                    out=std[:], in_=lv_of[j][:], func=ACT.Exp,
                    bias=shift[:, LV : LV + 1], scale=factor[:, LV : LV + 1],
                )
                std_of[j] = std

            def noise_block(j):
                noise = tail.tile([P, BLOCK], F32)
                nc.gpsimd.tensor_tensor(
                    out=noise[:], in0=std_of[j][:], in1=eps_t[:, block_cols(j)], op=ALU.mult
                )
                noise_of[j] = noise

            def sample_block(j):
                nc.vector.scalar_tensor_tensor(
                    out=z_less_shift[:, block_cols(j)], in0=m_of[j][:],
                    scalar=factor[:, M : M + 1], in1=noise_of[j][:],
                    op0=ALU.mult, op1=ALU.add, accum_out=z_sums[:, 0, j : j + 1],
                )

            def square_block(j):
                squares = tail.tile([P, BLOCK], F32)
                nc.scalar.activation(
                    out=squares[:], in_=z_less_shift[:, block_cols(j)], func=ACT.Square,
                    bias=shift[:, M : M + 1], accum_out=z_sums[:, 1, j : j + 1],
                )

            def transpose_back(source):
                back = psum.tile([P, SUB, D], F32, tag="bank")
                for s in range(SUB):
                    nc.tensor.transpose(back[:, s, :], source[:, s * P : (s + 1) * P], ident_f32[:])
                return back

            def store_z(j):
                back = transpose_back(z_less_shift[:, block_cols(j)])
                z_rows = staging.tile([P, SUB, D], F32)
                nc.vector.tensor_tensor(
                    out=z_rows[:], in0=back[:],
                    in1=shift_row[:].unsqueeze(1).to_broadcast([P, SUB, D]), op=ALU.add,
                )
                nc.sync.dma_start(
                    out=block_rows(out_0, j), in_=z_rows[:].rearrange("r s d -> r (s d)")
                )

            for j in range(NBLOCKS + 4):
                if j + 1 < NBLOCKS:
                    lv_of[j + 1] = head_product(LV, j + 1)
                if 1 <= j <= NBLOCKS:
                    m_of[j - 1] = head_product(M, j - 1)
                if j < NBLOCKS:
                    std_block(j)
                if 1 <= j <= NBLOCKS:
                    noise_block(j - 1)
                if 2 <= j <= NBLOCKS + 1:
                    sample_block(j - 2)
                if j >= 4:
                    square_block(j - 4)
                    store_z(j - 4)

            z_sum = small.tile([P, 2], F32)
            nc.vector.tensor_reduce(out=z_sum[:], in_=z_sums[:], axis=AXIS.X, op=ALU.add)
            z_mean = small.tile([P, 1], F32)
            nc.vector.tensor_scalar(
                out=z_mean[:], in0=z_sum[:, 0:1], scalar1=1.0 / ROWS, scalar2=shift[:, M : M + 1],
                op0=ALU.mult, op1=ALU.add,
            )
            z_mean2_less_eps = small.tile([P, 1], F32)
            nc.vector.tensor_scalar(
                out=z_mean2_less_eps[:], in0=z_mean[:], scalar1=z_mean[:], scalar2=BN_EPS,
                op0=ALU.mult, op1=ALU.subtract,
            )
            z_padded = small.tile([P, 1], F32)
            nc.vector.tensor_scalar(
                out=z_padded[:], in0=z_sum[:, 1:2], scalar1=1.0 / ROWS,
                scalar2=z_mean2_less_eps[:], op0=ALU.mult, op1=ALU.subtract,
            )
            z_factor = small.tile([P, 1], F32)
            nc.gpsimd.tensor_tensor(
                out=z_factor[:], in0=z_padded[:], in1=minus_half[:, 0:1], op=ALU.pow
            )
            zx_shift = small.tile([P, 1], F32)
            nc.vector.tensor_scalar(
                out=zx_shift[:], in0=z_sum[:, 0:1], scalar1=-1.0 / ROWS, scalar2=z_factor[:],
                op0=ALU.mult, op1=ALU.mult,
            )

            for j in range(NBLOCKS):
                zx_t = tail.tile([P, BLOCK], F32)
                nc.vector.tensor_scalar(
                    out=zx_t[:], in0=z_less_shift[:, block_cols(j)], scalar1=z_factor[:],
                    scalar2=zx_shift[:], op0=ALU.mult, op1=ALU.add,
                )
                back = transpose_back(zx_t[:])
                zx_rows = staging.tile([P, SUB * D], F32)
                nc.scalar.copy(out=zx_rows[:], in_=back[:].rearrange("r s d -> r (s d)"))
                nc.sync.dma_start(out=block_rows(out_1, j), in_=zx_rows[:])
